import numpy as np
import ml_dtypes

BF16 = ml_dtypes.bfloat16


def bf(x):
    return np.asarray(x, np.float32).astype(BF16)


def f32(x):
    return np.asarray(x, np.float32)


def f64(x):
    return np.asarray(x).astype(np.float64)


def striped(idx):
    return np.tile(idx.reshape(-1, 16).T, (8, 1))


C, S, N, T, B, K, O = 256, 512, 512, 2, 128, 1536, 512


def setup_inputs():
    return {"x": bf(np.random.standard_normal((C, S))), "w": bf(np.random.standard_normal((T, K, O)) / np.sqrt(K)), "offs": striped(np.random.permutation(S)[:N])}


def reference(x, w, offs):
    idx = offs[:16].T.reshape(-1)
    xs = f64(x)
    feat = np.concatenate([xs, xs * xs, xs[:, idx] * xs[:, :N]], axis=1)
    return (feat.reshape(T, B, K) @ f64(w)).reshape(C, O)

@@ -1,0 +1,90 @@
+import concourse.mybir as mybir
+from concourse.masks import make_identity
+
+BF16, F32, U16 = mybir.dt.bfloat16, mybir.dt.float32, mybir.dt.uint16
+MULT = mybir.AluOpType.mult
+
+P = 128
+T = 2
+S = 512
+N = 512
+O = 512
+BLOCKS = S // P
+SECTIONS = 3
+LIST_COLS = P // 16
+
+FLOPS = 2 * T * P * SECTIONS * S * O
+
+
+def tile_h_second_conv_kernel(tc, x, w, offs, out):
+    nc = tc.nc
+    with (
+        tc.tile_pool(name="held", bufs=1) as held,
+        tc.psum_pool(name="flips", bufs=1) as flips,
+        tc.psum_pool(name="sums", bufs=1) as sums,
+    ):
+        offsets = held.tile([P, N // 16], U16, name="offsets")
+        nc.sync.dma_start(offsets[:], offs)
+
+        x_rows = [held.tile([P, S], BF16, name=f"x_rows{t}") for t in range(T)]
+        for t in range(T):
+            nc.scalar.dma_start(x_rows[t][:], x[t * P : (t + 1) * P, :])
+
+        weights = [
+            [held.tile([P, BLOCKS, O], BF16, name=f"weights{t}_{sec}") for sec in range(SECTIONS)]
+            for t in range(T)
+        ]
+        for sec in range(SECTIONS):
+            for t in range(T):
+                nc.sync.dma_start(
+                    weights[t][sec][:],
+                    w[t, sec * S : (sec + 1) * S, :].rearrange("(b p) o -> p b o", p=P),
+                )
+
+        identity = held.tile([P, P], BF16, name="identity")
+        make_identity(nc, identity[:])
+
+        def flip(flipped, rows):
+            for b in range(BLOCKS):
+                block = slice(b * P, (b + 1) * P)
+                nc.tensor.transpose(flipped[:, block], rows[:, block], identity[:])
+
+        def accumulate(t, sec, features):
+            for b in range(BLOCKS):
+                nc.tensor.matmul(
+                    totals[t][:],
+                    features[:, b * P : (b + 1) * P],
+                    weights[t][sec][:, b, :],
+                    start=(sec == 0 and b == 0),
+                    stop=(sec == SECTIONS - 1 and b == BLOCKS - 1),
+                )
+
+        totals = [sums.tile([P, O], F32, name=f"totals{t}") for t in range(T)]
+
+        for t in range(T):
+            x_flip_psum = flips.tile([P, S], BF16, name=f"x_flip_psum{t}")
+            flip(x_flip_psum, x_rows[t])
+            x_flip = held.tile([P, S], BF16, name=f"x_flip{t}")
+            nc.vector.tensor_copy(x_flip[:], x_flip_psum[:])
+            square_flip = held.tile([P, S], BF16, name=f"square_flip{t}")
+            nc.scalar.square(square_flip[:], x_flip[:])
+            accumulate(t, 0, x_flip)
+            accumulate(t, 1, square_flip)
+
+        for t in range(T):
+            x_twin = held.tile([P, S], BF16, name=f"x_twin{t}")
+            nc.gpsimd.tensor_copy(x_twin[:], x_rows[t][:])
+            cross = held.tile([P, N], BF16, name=f"cross{t}")
+            for b in range(BLOCKS):
+                block = slice(b * P, (b + 1) * P)
+                picked = x_rows[t][:].indirect(offsets[:, b * LIST_COLS : (b + 1) * LIST_COLS])
+                nc.vector.tensor_tensor(cross[:, block], picked, x_twin[:, block], MULT)
+            cross_flip_psum = flips.tile([P, N], BF16, name=f"cross_flip_psum{t}")
+            flip(cross_flip_psum, cross)
+            cross_flip = held.tile([P, N], BF16, name=f"cross_flip{t}")
+            nc.vector.tensor_copy(cross_flip[:], cross_flip_psum[:])
+            accumulate(t, 2, cross_flip)
+
+            result = held.tile([P, O], F32, name=f"result{t}")
+            nc.scalar.copy(result[:], totals[t][:])
+            nc.sync.dma_start(out[t * P : (t + 1) * P, :], result[:])

@@ -10,44 +10,52 @@ S = 512
 N = 512
 O = 512
 BLOCKS = S // P
+VALUES, SQUARES, CROSS = 0, 1, 2
 SECTIONS = 3
 LIST_COLS = P // 16
 
 FLOPS = 2 * T * P * SECTIONS * S * O
+
+MATMUL_ORDER = ((0, VALUES), (0, SQUARES), (1, VALUES), (1, SQUARES), (0, CROSS), (1, CROSS))
 
 
 def tile_h_second_conv_kernel(tc, x, w, offs, out):
     nc = tc.nc
     with (
         tc.tile_pool(name="held", bufs=1) as held,
-        tc.psum_pool(name="flips", bufs=1) as flips,
+        tc.psum_pool(name="flips", bufs=2) as flips,
         tc.psum_pool(name="sums", bufs=1) as sums,
     ):
+        x_rows = [held.tile([P, S], BF16, name=f"x_rows{t}") for t in range(T)]
+        nc.sync.dma_start(x_rows[0][:], x[0:P, :])
+        nc.scalar.dma_start(x_rows[1][:], x[P : 2 * P, :])
+
         offsets = held.tile([P, N // 16], U16, name="offsets")
         nc.sync.dma_start(offsets[:], offs)
-
-        x_rows = [held.tile([P, S], BF16, name=f"x_rows{t}") for t in range(T)]
-        for t in range(T):
-            nc.scalar.dma_start(x_rows[t][:], x[t * P : (t + 1) * P, :])
 
         weights = [
             [held.tile([P, BLOCKS, O], BF16, name=f"weights{t}_{sec}") for sec in range(SECTIONS)]
             for t in range(T)
         ]
-        for sec in range(SECTIONS):
-            for t in range(T):
+        for t, sec in MATMUL_ORDER:
+            for b in range(0, BLOCKS, 2):
+                first_row = sec * S + b * P
                 nc.sync.dma_start(
-                    weights[t][sec][:],
-                    w[t, sec * S : (sec + 1) * S, :].rearrange("(b p) o -> p b o", p=P),
+                    weights[t][sec][:, b : b + 2, :],
+                    w[t, first_row : first_row + 2 * P, :].rearrange("(b p) o -> p b o", p=P),
                 )
 
         identity = held.tile([P, P], BF16, name="identity")
         make_identity(nc, identity[:])
 
-        def flip(flipped, rows):
+        totals = [sums.tile([P, O], F32, name=f"totals{t}") for t in range(T)]
+
+        def flip(rows):
+            flip_in_psum = flips.tile([P, S], BF16, name="flip_in_psum")
             for b in range(BLOCKS):
                 block = slice(b * P, (b + 1) * P)
-                nc.tensor.transpose(flipped[:, block], rows[:, block], identity[:])
+                nc.tensor.transpose(flip_in_psum[:, block], rows[:, block], identity[:])
+            return flip_in_psum
 
         def accumulate(t, sec, features):
             for b in range(BLOCKS):
@@ -55,36 +63,42 @@ def tile_h_second_conv_kernel(tc, x, w, offs, out):
                     totals[t][:],
                     features[:, b * P : (b + 1) * P],
                     weights[t][sec][:, b, :],
-                    start=(sec == 0 and b == 0),
-                    stop=(sec == SECTIONS - 1 and b == BLOCKS - 1),
+                    start=(sec == VALUES and b == 0),
+                    stop=(sec == CROSS and b == BLOCKS - 1),
                 )
 
-        totals = [sums.tile([P, O], F32, name=f"totals{t}") for t in range(T)]
-
+        x_flipped = [held.tile([P, S], BF16, name=f"x_flipped{t}") for t in range(T)]
+        squares_flipped = [held.tile([P, S], BF16, name=f"squares_flipped{t}") for t in range(T)]
         for t in range(T):
-            x_flip_psum = flips.tile([P, S], BF16, name=f"x_flip_psum{t}")
-            flip(x_flip_psum, x_rows[t])
-            x_flip = held.tile([P, S], BF16, name=f"x_flip{t}")
-            nc.vector.tensor_copy(x_flip[:], x_flip_psum[:])
-            square_flip = held.tile([P, S], BF16, name=f"square_flip{t}")
-            nc.scalar.square(square_flip[:], x_flip[:])
-            accumulate(t, 0, x_flip)
-            accumulate(t, 1, square_flip)
+            x_in_psum = flip(x_rows[t])
+            nc.scalar.copy(x_flipped[t][:], x_in_psum[:])
+            nc.scalar.square(squares_flipped[t][:], x_in_psum[:])
 
+        cross = [held.tile([P, N], BF16, name=f"cross{t}") for t in range(T)]
         for t in range(T):
             x_twin = held.tile([P, S], BF16, name=f"x_twin{t}")
             nc.gpsimd.tensor_copy(x_twin[:], x_rows[t][:])
-            cross = held.tile([P, N], BF16, name=f"cross{t}")
             for b in range(BLOCKS):
                 block = slice(b * P, (b + 1) * P)
                 picked = x_rows[t][:].indirect(offsets[:, b * LIST_COLS : (b + 1) * LIST_COLS])
-                nc.vector.tensor_tensor(cross[:, block], picked, x_twin[:, block], MULT)
-            cross_flip_psum = flips.tile([P, N], BF16, name=f"cross_flip_psum{t}")
-            flip(cross_flip_psum, cross)
-            cross_flip = held.tile([P, N], BF16, name=f"cross_flip{t}")
-            nc.vector.tensor_copy(cross_flip[:], cross_flip_psum[:])
-            accumulate(t, 2, cross_flip)
+                nc.vector.tensor_tensor(cross[t][:, block], picked, x_twin[:, block], MULT)
 
-            result = held.tile([P, O], F32, name=f"result{t}")
-            nc.scalar.copy(result[:], totals[t][:])
-            nc.sync.dma_start(out[t * P : (t + 1) * P, :], result[:])
+        def flip_cross(t):
+            cross_flipped = held.tile([P, N], BF16, name=f"cross_flipped{t}")
+            nc.scalar.copy(cross_flipped[:], flip(cross[t])[:])
+            return cross_flipped
+
+        accumulate(0, VALUES, x_flipped[0])
+        accumulate(0, SQUARES, squares_flipped[0])
+        cross_flipped0 = flip_cross(0)
+        accumulate(1, VALUES, x_flipped[1])
+        cross_flipped1 = flip_cross(1)
+        accumulate(1, SQUARES, squares_flipped[1])
+        accumulate(0, CROSS, cross_flipped0)
+        accumulate(1, CROSS, cross_flipped1)
+
+        result = [held.tile([P, O], F32, name=f"result{t}") for t in range(T)]
+        nc.scalar.copy(result[0][:], totals[0][:])
+        nc.scalar.dma_start(out[0:P, :], result[0][:])
+        nc.vector.tensor_copy(result[1][:], totals[1][:])
+        nc.sync.dma_start(out[P : 2 * P, :], result[1][:])

@@ -13,6 +13,9 @@ BLOCKS = S // P
 VALUES, SQUARES, CROSS = 0, 1, 2
 SECTIONS = 3
 LIST_COLS = P // 16
+UNIT = 2 * P
+UNITS = S // UNIT
+GROUP = O // 2
 
 FLOPS = 2 * T * P * SECTIONS * S * O
 
@@ -23,7 +26,7 @@ def tile_h_second_conv_kernel(tc, x, w, offs, out):
     nc = tc.nc
     with (
         tc.tile_pool(name="held", bufs=1) as held,
-        tc.psum_pool(name="flips", bufs=2) as flips,
+        tc.psum_pool(name="flips", bufs=4) as flips,
         tc.psum_pool(name="sums", bufs=1) as sums,
     ):
         x_rows = [held.tile([P, S], BF16, name=f"x_rows{t}") for t in range(T)]
@@ -38,41 +41,55 @@ def tile_h_second_conv_kernel(tc, x, w, offs, out):
             for t in range(T)
         ]
         for t, sec in MATMUL_ORDER:
-            for b in range(0, BLOCKS, 2):
-                first_row = sec * S + b * P
+            for u in range(UNITS):
+                first_row = sec * S + u * UNIT
                 nc.sync.dma_start(
-                    weights[t][sec][:, b : b + 2, :],
-                    w[t, first_row : first_row + 2 * P, :].rearrange("(b p) o -> p b o", p=P),
+                    weights[t][sec][:, 2 * u : 2 * u + 2, :],
+                    w[t, first_row : first_row + UNIT, :].rearrange("(b p) o -> p b o", p=P),
                 )
 
         identity = held.tile([P, P], BF16, name="identity")
         make_identity(nc, identity[:])
 
-        totals = [sums.tile([P, O], F32, name=f"totals{t}") for t in range(T)]
+        totals = [[sums.tile([P, GROUP], F32, name=f"totals{t}_{g}") for g in range(2)] for t in range(T)]
 
-        def flip(rows):
-            flip_in_psum = flips.tile([P, S], BF16, name="flip_in_psum")
-            for b in range(BLOCKS):
-                block = slice(b * P, (b + 1) * P)
-                nc.tensor.transpose(flip_in_psum[:, block], rows[:, block], identity[:])
+        def flip(rows, u):
+            flip_in_psum = flips.tile([P, UNIT], BF16, name="flip_in_psum")
+            for i in range(2):
+                nc.tensor.transpose(
+                    flip_in_psum[:, i * P : (i + 1) * P],
+                    rows[:, u * UNIT + i * P : u * UNIT + (i + 1) * P],
+                    identity[:],
+                )
             return flip_in_psum
 
         def accumulate(t, sec, features):
-            for b in range(BLOCKS):
-                nc.tensor.matmul(
-                    totals[t][:],
-                    features[:, b * P : (b + 1) * P],
-                    weights[t][sec][:, b, :],
-                    start=(sec == VALUES and b == 0),
-                    stop=(sec == CROSS and b == BLOCKS - 1),
-                )
+            for u in range(UNITS):
+                for g in range(2):
+                    for b in (2 * u, 2 * u + 1):
+                        nc.tensor.matmul(
+                            totals[t][g][:],
+                            features[:, b * P : (b + 1) * P],
+                            weights[t][sec][:, b, g * GROUP : (g + 1) * GROUP],
+                            start=(sec == VALUES and b == 0),
+                            stop=(sec == CROSS and b == BLOCKS - 1),
+                        )
 
+        def store(t):
+            result = [held.tile([P, GROUP], F32, name=f"result{t}_{g}") for g in range(2)]
+            nc.vector.tensor_copy(result[0][:], totals[t][0][:])
+            nc.sync.dma_start(out[t * P : (t + 1) * P, 0:GROUP], result[0][:])
+            nc.scalar.copy(result[1][:], totals[t][1][:])
+            nc.scalar.dma_start(out[t * P : (t + 1) * P, GROUP:O], result[1][:])
+
+        x_in_psum = [[flip(x_rows[t], u) for u in range(UNITS)] for t in range(T)]
         x_flipped = [held.tile([P, S], BF16, name=f"x_flipped{t}") for t in range(T)]
         squares_flipped = [held.tile([P, S], BF16, name=f"squares_flipped{t}") for t in range(T)]
         for t in range(T):
-            x_in_psum = flip(x_rows[t])
-            nc.scalar.copy(x_flipped[t][:], x_in_psum[:])
-            nc.scalar.square(squares_flipped[t][:], x_in_psum[:])
+            for u in range(UNITS):
+                nc.scalar.copy(x_flipped[t][:, u * UNIT : (u + 1) * UNIT], x_in_psum[t][u][:])
+            for u in range(UNITS):
+                nc.scalar.square(squares_flipped[t][:, u * UNIT : (u + 1) * UNIT], x_in_psum[t][u][:])
 
         cross = [held.tile([P, N], BF16, name=f"cross{t}") for t in range(T)]
         for t in range(T):
@@ -85,7 +102,8 @@ def tile_h_second_conv_kernel(tc, x, w, offs, out):
 
         def flip_cross(t):
             cross_flipped = held.tile([P, N], BF16, name=f"cross_flipped{t}")
-            nc.scalar.copy(cross_flipped[:], flip(cross[t])[:])
+            for u in range(UNITS):
+                nc.scalar.copy(cross_flipped[:, u * UNIT : (u + 1) * UNIT], flip(cross[t], u)[:])
             return cross_flipped
 
         accumulate(0, VALUES, x_flipped[0])
@@ -95,10 +113,6 @@ def tile_h_second_conv_kernel(tc, x, w, offs, out):
         cross_flipped1 = flip_cross(1)
         accumulate(1, SQUARES, squares_flipped[1])
         accumulate(0, CROSS, cross_flipped0)
+        store(0)
         accumulate(1, CROSS, cross_flipped1)
-
-        result = [held.tile([P, O], F32, name=f"result{t}") for t in range(T)]
-        nc.scalar.copy(result[0][:], totals[0][:])
-        nc.scalar.dma_start(out[0:P, :], result[0][:])
-        nc.vector.tensor_copy(result[1][:], totals[1][:])
-        nc.sync.dma_start(out[P : 2 * P, :], result[1][:])
+        store(1)

@@ -20,6 +20,7 @@ GROUP = O // 2
 FLOPS = 2 * T * P * SECTIONS * S * O
 
 MATMUL_ORDER = ((0, VALUES), (0, SQUARES), (1, VALUES), (1, SQUARES), (0, CROSS), (1, CROSS))
+WARMING_MATMULS = 6
 
 
 def tile_h_second_conv_kernel(tc, x, w, offs, out):
@@ -48,10 +49,16 @@ def tile_h_second_conv_kernel(tc, x, w, offs, out):
                     w[t, first_row : first_row + UNIT, :].rearrange("(b p) o -> p b o", p=P),
                 )
 
+        zeros = held.tile([P, GROUP], BF16, name="zeros")
+        nc.gpsimd.memset(zeros[:], 0.0)
+
         identity = held.tile([P, P], BF16, name="identity")
         make_identity(nc, identity[:])
 
         totals = [[sums.tile([P, GROUP], F32, name=f"totals{t}_{g}") for g in range(2)] for t in range(T)]
+
+        for i in range(WARMING_MATMULS):
+            nc.tensor.matmul(totals[T - 1][1][:], zeros[:, 0:P], zeros[:], start=True, stop=True)
 
         def flip(rows, u):
             flip_in_psum = flips.tile([P, UNIT], BF16, name="flip_in_psum")

@@ -20,7 +20,6 @@ GROUP = O // 2
 FLOPS = 2 * T * P * SECTIONS * S * O
 
 MATMUL_ORDER = ((0, VALUES), (0, SQUARES), (1, VALUES), (1, SQUARES), (0, CROSS), (1, CROSS))
-WARMING_MATMULS = 6
 
 
 def tile_h_second_conv_kernel(tc, x, w, offs, out):
@@ -42,32 +41,23 @@ def tile_h_second_conv_kernel(tc, x, w, offs, out):
             for t in range(T)
         ]
         for t, sec in MATMUL_ORDER:
-            for u in range(UNITS):
-                first_row = sec * S + u * UNIT
-                nc.sync.dma_start(
-                    weights[t][sec][:, 2 * u : 2 * u + 2, :],
-                    w[t, first_row : first_row + UNIT, :].rearrange("(b p) o -> p b o", p=P),
-                )
-
-        zeros = held.tile([P, GROUP], BF16, name="zeros")
-        nc.gpsimd.memset(zeros[:], 0.0)
+            section = w[t, sec * S : (sec + 1) * S, :].rearrange("(p b) o -> p b o", b=BLOCKS)
+            if (t, sec) in (MATMUL_ORDER[0], MATMUL_ORDER[-1]):
+                for u in range(UNITS):
+                    nc.sync.dma_start(weights[t][sec][:, 2 * u : 2 * u + 2, :], section[:, 2 * u : 2 * u + 2, :])
+            else:
+                nc.sync.dma_start(weights[t][sec][:], section)
 
         identity = held.tile([P, P], BF16, name="identity")
         make_identity(nc, identity[:])
 
         totals = [[sums.tile([P, GROUP], F32, name=f"totals{t}_{g}") for g in range(2)] for t in range(T)]
 
-        for i in range(WARMING_MATMULS):
-            nc.tensor.matmul(totals[T - 1][1][:], zeros[:, 0:P], zeros[:], start=True, stop=True)
-
         def flip(rows, u):
+            every_fourth = rows[:].rearrange("r (p b) -> r b p", b=BLOCKS)
             flip_in_psum = flips.tile([P, UNIT], BF16, name="flip_in_psum")
             for i in range(2):
-                nc.tensor.transpose(
-                    flip_in_psum[:, i * P : (i + 1) * P],
-                    rows[:, u * UNIT + i * P : u * UNIT + (i + 1) * P],
-                    identity[:],
-                )
+                nc.tensor.transpose(flip_in_psum[:, i * P : (i + 1) * P], every_fourth[:, 2 * u + i, :], identity[:])
             return flip_in_psum
 
         def accumulate(t, sec, features):

@@ -20,6 +20,7 @@ GROUP = O // 2
 FLOPS = 2 * T * P * SECTIONS * S * O
 
 MATMUL_ORDER = ((0, VALUES), (0, SQUARES), (1, VALUES), (1, SQUARES), (0, CROSS), (1, CROSS))
+WARMING_MATMULS = 6
 
 
 def tile_h_second_conv_kernel(tc, x, w, offs, out):
@@ -48,10 +49,16 @@ def tile_h_second_conv_kernel(tc, x, w, offs, out):
             else:
                 nc.sync.dma_start(weights[t][sec][:], section)
 
+        zeros = held.tile([P, GROUP], BF16, name="zeros")
+        nc.gpsimd.memset(zeros[:], 0.0)
+
         identity = held.tile([P, P], BF16, name="identity")
         make_identity(nc, identity[:])
 
         totals = [[sums.tile([P, GROUP], F32, name=f"totals{t}_{g}") for g in range(2)] for t in range(T)]
+
+        for i in range(WARMING_MATMULS):
+            nc.tensor.matmul(totals[T - 1][1][:], zeros[:, 0:P], zeros[:], start=True, stop=True)
 
         def flip(rows, u):
             every_fourth = rows[:].rearrange("r (p b) -> r b p", b=BLOCKS)

@@ -20,7 +20,7 @@ GROUP = O // 2
 FLOPS = 2 * T * P * SECTIONS * S * O
 
 MATMUL_ORDER = ((0, VALUES), (0, SQUARES), (1, VALUES), (1, SQUARES), (0, CROSS), (1, CROSS))
-WARMING_MATMULS = 6
+WARMING_MATMULS = 10
 
 
 def tile_h_second_conv_kernel(tc, x, w, offs, out):

import concourse.mybir as mybir
from concourse.masks import make_identity

BF16, F32, U16 = mybir.dt.bfloat16, mybir.dt.float32, mybir.dt.uint16
MULT = mybir.AluOpType.mult

P = 128
T = 2
S = 512
N = 512
O = 512
BLOCKS = S // P
VALUES, SQUARES, CROSS = 0, 1, 2
SECTIONS = 3
LIST_COLS = P // 16
UNIT = 2 * P
UNITS = S // UNIT
GROUP = O // 2

FLOPS = 2 * T * P * SECTIONS * S * O

MATMUL_ORDER = ((0, VALUES), (0, SQUARES), (1, VALUES), (1, SQUARES), (0, CROSS), (1, CROSS))
WARMING_MATMULS = 10


def tile_h_second_conv_kernel(tc, x, w, offs, out):
    nc = tc.nc
    with (
        tc.tile_pool(name="held", bufs=1) as held,
        tc.psum_pool(name="flips", bufs=4) as flips,
        tc.psum_pool(name="sums", bufs=1) as sums,
    ):
        x_rows = [held.tile([P, S], BF16, name=f"x_rows{t}") for t in range(T)]
        nc.sync.dma_start(x_rows[0][:], x[0:P, :])
        nc.scalar.dma_start(x_rows[1][:], x[P : 2 * P, :])

        offsets = held.tile([P, N // 16], U16, name="offsets")
        nc.sync.dma_start(offsets[:], offs)

        weights = [
            [held.tile([P, BLOCKS, O], BF16, name=f"weights{t}_{sec}") for sec in range(SECTIONS)]
            for t in range(T)
        ]
        for t, sec in MATMUL_ORDER:
            section = w[t, sec * S : (sec + 1) * S, :].rearrange("(p b) o -> p b o", b=BLOCKS)
            if (t, sec) in (MATMUL_ORDER[0], MATMUL_ORDER[-1]):
                for u in range(UNITS):
                    nc.sync.dma_start(weights[t][sec][:, 2 * u : 2 * u + 2, :], section[:, 2 * u : 2 * u + 2, :])
            else:
                nc.sync.dma_start(weights[t][sec][:], section)

        zeros = held.tile([P, GROUP], BF16, name="zeros")
        nc.gpsimd.memset(zeros[:], 0.0)

        identity = held.tile([P, P], BF16, name="identity")
        make_identity(nc, identity[:])

        totals = [[sums.tile([P, GROUP], F32, name=f"totals{t}_{g}") for g in range(2)] for t in range(T)]

        for i in range(WARMING_MATMULS):
            nc.tensor.matmul(totals[T - 1][1][:], zeros[:, 0:P], zeros[:], start=True, stop=True)

        def flip(rows, u):
            every_fourth = rows[:].rearrange("r (p b) -> r b p", b=BLOCKS)
            flip_in_psum = flips.tile([P, UNIT], BF16, name="flip_in_psum")
            for i in range(2):
                nc.tensor.transpose(flip_in_psum[:, i * P : (i + 1) * P], every_fourth[:, 2 * u + i, :], identity[:])
            return flip_in_psum

        def accumulate(t, sec, features):
            for u in range(UNITS):
                for g in range(2):
                    for b in (2 * u, 2 * u + 1):
                        nc.tensor.matmul(
                            totals[t][g][:],
                            features[:, b * P : (b + 1) * P],
                            weights[t][sec][:, b, g * GROUP : (g + 1) * GROUP],
                            start=(sec == VALUES and b == 0),
                            stop=(sec == CROSS and b == BLOCKS - 1),
                        )

        def store(t):
            result = [held.tile([P, GROUP], F32, name=f"result{t}_{g}") for g in range(2)]
            nc.vector.tensor_copy(result[0][:], totals[t][0][:])
            nc.sync.dma_start(out[t * P : (t + 1) * P, 0:GROUP], result[0][:])
            nc.scalar.copy(result[1][:], totals[t][1][:])
            nc.scalar.dma_start(out[t * P : (t + 1) * P, GROUP:O], result[1][:])

        x_in_psum = [[flip(x_rows[t], u) for u in range(UNITS)] for t in range(T)]
        x_flipped = [held.tile([P, S], BF16, name=f"x_flipped{t}") for t in range(T)]
        squares_flipped = [held.tile([P, S], BF16, name=f"squares_flipped{t}") for t in range(T)]
        for t in range(T):
            for u in range(UNITS):
                nc.scalar.copy(x_flipped[t][:, u * UNIT : (u + 1) * UNIT], x_in_psum[t][u][:])
            for u in range(UNITS):
                nc.scalar.square(squares_flipped[t][:, u * UNIT : (u + 1) * UNIT], x_in_psum[t][u][:])

        cross = [held.tile([P, N], BF16, name=f"cross{t}") for t in range(T)]
        for t in range(T):
            x_twin = held.tile([P, S], BF16, name=f"x_twin{t}")
            nc.gpsimd.tensor_copy(x_twin[:], x_rows[t][:])
            for b in range(BLOCKS):
                block = slice(b * P, (b + 1) * P)
                picked = x_rows[t][:].indirect(offsets[:, b * LIST_COLS : (b + 1) * LIST_COLS])
                nc.vector.tensor_tensor(cross[t][:, block], picked, x_twin[:, block], MULT)

        def flip_cross(t):
            cross_flipped = held.tile([P, N], BF16, name=f"cross_flipped{t}")
            for u in range(UNITS):
                nc.scalar.copy(cross_flipped[:, u * UNIT : (u + 1) * UNIT], flip(cross[t], u)[:])
            return cross_flipped

        accumulate(0, VALUES, x_flipped[0])
        accumulate(0, SQUARES, squares_flipped[0])
        cross_flipped0 = flip_cross(0)
        accumulate(1, VALUES, x_flipped[1])
        cross_flipped1 = flip_cross(1)
        accumulate(1, SQUARES, squares_flipped[1])
        accumulate(0, CROSS, cross_flipped0)
        store(0)
        accumulate(1, CROSS, cross_flipped1)
        store(1)
